import numpy as np
import ml_dtypes

BF16 = ml_dtypes.bfloat16


def bf(x):
    return np.asarray(x, np.float32).astype(BF16)


def f32(x):
    return np.asarray(x, np.float32)


def f64(x):
    return np.asarray(x).astype(np.float64)


def striped(idx):
    return np.tile(idx.reshape(-1, 16).T, (8, 1))


D, S, M, N, L = 128, 1024, 256, 1024, 4


def sigmoid(v):
    return 1.0 / (1.0 + np.exp(-v))


def setup_inputs():
    return {"table": bf(np.random.standard_normal((D, S))), "words": bf(1.5 * np.random.standard_normal((D, M)) / np.sqrt(D)), "sgn": f32(np.where(np.random.random((M, N)) < 0.5, -1.0, 1.0)), "offs": striped(np.random.permutation(np.tile(np.arange(S), 2))[:N])}


def reference(table, words, sgn, offs):
    idx = offs[:16].T.reshape(-1)
    scores = f64(words).T @ f64(table)[:, idx]
    p = sigmoid(f64(sgn) * scores)
    return p.reshape(M, N // L, L).prod(axis=-1)

@@ -1,0 +1,63 @@
+import concourse.mybir as mybir
+
+P = 128
+NODES = 1024
+WORDS = 256
+ENTRIES = 1024
+STEPS = 4
+PIECE = 512
+PATHS = PIECE // STEPS
+
+FLOPS = 2 * P * WORDS * ENTRIES
+
+BF16 = mybir.dt.bfloat16
+F32 = mybir.dt.float32
+U16 = mybir.dt.uint16
+MULT = mybir.AluOpType.mult
+SIGMOID = mybir.ActivationFunctionType.Sigmoid
+
+
+def tile_huffmantree_kernel(tc, table, words, sgn, offs, out):
+    nc = tc.nc
+    with (
+        tc.tile_pool(name="held", bufs=1) as held,
+        tc.tile_pool(name="work", bufs=4) as work,
+        tc.psum_pool(name="psum", bufs=4) as psum,
+    ):
+        offsets = held.tile([P, ENTRIES // 16], U16, name="offsets")
+        nc.sync.dma_start(offsets[:], offs)
+        nodes = held.tile([P, NODES], BF16, name="nodes")
+        nc.sync.dma_start(nodes[:], table)
+        vectors = held.tile([P, WORDS], BF16, name="vectors")
+        nc.sync.dma_start(vectors[:], words)
+
+        for block in range(WORDS // P):
+            rows = slice(block * P, (block + 1) * P)
+            for piece in range(ENTRIES // PIECE):
+                sign = work.tile([P, PIECE], F32, name="sign")
+                nc.sync.dma_start(sign[:], sgn[rows, piece * PIECE : (piece + 1) * PIECE])
+
+                score = psum.tile([P, PIECE], F32, name="score")
+                nc.tensor.matmul(
+                    score[:],
+                    vectors[:, rows],
+                    nodes[:].indirect(offsets[:, piece * (PIECE // 16) : (piece + 1) * (PIECE // 16)]),
+                    start=True,
+                    stop=True,
+                )
+
+                signed = work.tile([P, PIECE], F32, name="signed")
+                nc.vector.tensor_tensor(signed[:], score[:], sign[:], MULT)
+
+                prob = work.tile([P, PATHS, STEPS], F32, name="prob")
+                nc.scalar.activation(prob[:].rearrange("p t l -> p (t l)"), signed[:], SIGMOID)
+
+                half = work.tile([P, PATHS, 2], F32, name="half")
+                nc.vector.tensor_tensor(half[:], prob[:, :, 0:2], prob[:, :, 2:4], MULT)
+                path = work.tile([P, PATHS, 1], F32, name="path")
+                nc.vector.tensor_tensor(path[:], half[:, :, 0:1], half[:, :, 1:2], MULT)
+
+                nc.sync.dma_start(
+                    out[rows, piece * PATHS : (piece + 1) * PATHS],
+                    path[:].rearrange("p t l -> p (t l)"),
+                )

@@ -7,6 +7,7 @@ ENTRIES = 1024
 STEPS = 4
 PIECE = 512
 PATHS = PIECE // STEPS
+WARMUPS = 6
 
 FLOPS = 2 * P * WORDS * ENTRIES
 
@@ -30,6 +31,12 @@ def tile_huffmantree_kernel(tc, table, words, sgn, offs, out):
         nc.sync.dma_start(nodes[:], table)
         vectors = held.tile([P, WORDS], BF16, name="vectors")
         nc.sync.dma_start(vectors[:], words)
+
+        zeros = held.tile([P, PIECE], BF16, name="zeros")
+        nc.vector.memset(zeros[:], 0.0)
+        unused = psum.tile([P, PIECE], F32, name="unused")
+        for _ in range(WARMUPS):
+            nc.tensor.matmul(unused[:], zeros[:, 0:P], zeros[:], start=True, stop=True)
 
         for block in range(WORDS // P):
             rows = slice(block * P, (block + 1) * P)

@@ -7,7 +7,6 @@ ENTRIES = 1024
 STEPS = 4
 PIECE = 512
 PATHS = PIECE // STEPS
-WARMUPS = 6
 
 FLOPS = 2 * P * WORDS * ENTRIES
 
@@ -28,21 +27,16 @@ def tile_huffmantree_kernel(tc, table, words, sgn, offs, out):
         offsets = held.tile([P, ENTRIES // 16], U16, name="offsets")
         nc.sync.dma_start(offsets[:], offs)
         nodes = held.tile([P, NODES], BF16, name="nodes")
-        nc.sync.dma_start(nodes[:], table)
+        nc.scalar.dma_start(nodes[:], table)
         vectors = held.tile([P, WORDS], BF16, name="vectors")
         nc.sync.dma_start(vectors[:], words)
-
-        zeros = held.tile([P, PIECE], BF16, name="zeros")
-        nc.vector.memset(zeros[:], 0.0)
-        unused = psum.tile([P, PIECE], F32, name="unused")
-        for _ in range(WARMUPS):
-            nc.tensor.matmul(unused[:], zeros[:, 0:P], zeros[:], start=True, stop=True)
 
         for block in range(WORDS // P):
             rows = slice(block * P, (block + 1) * P)
             for piece in range(ENTRIES // PIECE):
                 sign = work.tile([P, PIECE], F32, name="sign")
-                nc.sync.dma_start(sign[:], sgn[rows, piece * PIECE : (piece + 1) * PIECE])
+                queue = nc.sync if piece % 2 == 0 else nc.scalar
+                queue.dma_start(sign[:], sgn[rows, piece * PIECE : (piece + 1) * PIECE])
 
                 score = psum.tile([P, PIECE], F32, name="score")
                 nc.tensor.matmul(

@@ -7,6 +7,7 @@ ENTRIES = 1024
 STEPS = 4
 PIECE = 512
 PATHS = PIECE // STEPS
+WARMUPS = 3
 
 FLOPS = 2 * P * WORDS * ENTRIES
 
@@ -27,16 +28,21 @@ def tile_huffmantree_kernel(tc, table, words, sgn, offs, out):
         offsets = held.tile([P, ENTRIES // 16], U16, name="offsets")
         nc.sync.dma_start(offsets[:], offs)
         nodes = held.tile([P, NODES], BF16, name="nodes")
-        nc.scalar.dma_start(nodes[:], table)
+        nc.sync.dma_start(nodes[:], table)
         vectors = held.tile([P, WORDS], BF16, name="vectors")
         nc.sync.dma_start(vectors[:], words)
+
+        zeros = held.tile([P, 512], BF16, name="zeros")
+        nc.vector.memset(zeros[:], 0.0)
+        unused = psum.tile([P, 512], F32, name="unused")
+        for _ in range(WARMUPS):
+            nc.tensor.matmul(unused[:], zeros[:, 0:P], zeros[:], start=True, stop=True)
 
         for block in range(WORDS // P):
             rows = slice(block * P, (block + 1) * P)
             for piece in range(ENTRIES // PIECE):
                 sign = work.tile([P, PIECE], F32, name="sign")
-                queue = nc.sync if piece % 2 == 0 else nc.scalar
-                queue.dma_start(sign[:], sgn[rows, piece * PIECE : (piece + 1) * PIECE])
+                nc.sync.dma_start(sign[:], sgn[rows, piece * PIECE : (piece + 1) * PIECE])
 
                 score = psum.tile([P, PIECE], F32, name="score")
                 nc.tensor.matmul(
@@ -53,10 +59,13 @@ def tile_huffmantree_kernel(tc, table, words, sgn, offs, out):
                 prob = work.tile([P, PATHS, STEPS], F32, name="prob")
                 nc.scalar.activation(prob[:].rearrange("p t l -> p (t l)"), signed[:], SIGMOID)
 
-                half = work.tile([P, PATHS, 2], F32, name="half")
-                nc.vector.tensor_tensor(half[:], prob[:, :, 0:2], prob[:, :, 2:4], MULT)
                 path = work.tile([P, PATHS, 1], F32, name="path")
-                nc.vector.tensor_tensor(path[:], half[:, :, 0:1], half[:, :, 1:2], MULT)
+                if block == 0:
+                    half = work.tile([P, PATHS, 2], F32, name="half")
+                    nc.gpsimd.tensor_tensor(half[:], prob[:, :, 0:2], prob[:, :, 2:4], MULT)
+                    nc.gpsimd.tensor_tensor(path[:], half[:, :, 0:1], half[:, :, 1:2], MULT)
+                else:
+                    nc.vector.tensor_reduce(path[:], prob[:], mybir.AxisListType.X, MULT)
 
                 nc.sync.dma_start(
                     out[rows, piece * PATHS : (piece + 1) * PATHS],

@@ -5,9 +5,7 @@ NODES = 1024
 WORDS = 256
 ENTRIES = 1024
 STEPS = 4
-PIECE = 512
-PATHS = PIECE // STEPS
-WARMUPS = 3
+PIECE = (512, 256)
 
 FLOPS = 2 * P * WORDS * ENTRIES
 
@@ -22,52 +20,48 @@ def tile_huffmantree_kernel(tc, table, words, sgn, offs, out):
     nc = tc.nc
     with (
         tc.tile_pool(name="held", bufs=1) as held,
-        tc.tile_pool(name="work", bufs=4) as work,
-        tc.psum_pool(name="psum", bufs=4) as psum,
+        tc.tile_pool(name="work", bufs=6) as work,
+        tc.psum_pool(name="psum", bufs=6) as psum,
     ):
-        offsets = held.tile([P, ENTRIES // 16], U16, name="offsets")
-        nc.sync.dma_start(offsets[:], offs)
         nodes = held.tile([P, NODES], BF16, name="nodes")
         nc.sync.dma_start(nodes[:], table)
         vectors = held.tile([P, WORDS], BF16, name="vectors")
         nc.sync.dma_start(vectors[:], words)
-
-        zeros = held.tile([P, 512], BF16, name="zeros")
-        nc.vector.memset(zeros[:], 0.0)
-        unused = psum.tile([P, 512], F32, name="unused")
-        for _ in range(WARMUPS):
-            nc.tensor.matmul(unused[:], zeros[:, 0:P], zeros[:], start=True, stop=True)
+        offsets = held.tile([P, ENTRIES // 16], U16, name="offsets")
+        nc.sync.dma_start(offsets[:], offs)
 
         for block in range(WORDS // P):
             rows = slice(block * P, (block + 1) * P)
-            for piece in range(ENTRIES // PIECE):
-                sign = work.tile([P, PIECE], F32, name="sign")
-                nc.sync.dma_start(sign[:], sgn[rows, piece * PIECE : (piece + 1) * PIECE])
+            entries = PIECE[block]
+            paths = entries // STEPS
+            for first in range(0, ENTRIES, entries):
+                sign = work.tile([P, entries], F32, name="sign")
+                nc.sync.dma_start(sign[:], sgn[rows, first : first + entries])
 
-                score = psum.tile([P, PIECE], F32, name="score")
+                score = psum.tile([P, entries], F32, name="score")
                 nc.tensor.matmul(
                     score[:],
                     vectors[:, rows],
-                    nodes[:].indirect(offsets[:, piece * (PIECE // 16) : (piece + 1) * (PIECE // 16)]),
+                    nodes[:].indirect(offsets[:, first // 16 : (first + entries) // 16]),
                     start=True,
                     stop=True,
                 )
 
-                signed = work.tile([P, PIECE], F32, name="signed")
+                signed = work.tile([P, entries], F32, name="signed")
                 nc.vector.tensor_tensor(signed[:], score[:], sign[:], MULT)
 
-                prob = work.tile([P, PATHS, STEPS], F32, name="prob")
+                prob = work.tile([P, paths, STEPS], F32, name="prob")
                 nc.scalar.activation(prob[:].rearrange("p t l -> p (t l)"), signed[:], SIGMOID)
 
-                path = work.tile([P, PATHS, 1], F32, name="path")
+                path = work.tile([P, paths, 1], F32, name="path")
                 if block == 0:
-                    half = work.tile([P, PATHS, 2], F32, name="half")
+                    half = work.tile([P, paths, 2], F32, name="half")
                     nc.gpsimd.tensor_tensor(half[:], prob[:, :, 0:2], prob[:, :, 2:4], MULT)
                     nc.gpsimd.tensor_tensor(path[:], half[:, :, 0:1], half[:, :, 1:2], MULT)
                 else:
                     nc.vector.tensor_reduce(path[:], prob[:], mybir.AxisListType.X, MULT)
 
                 nc.sync.dma_start(
-                    out[rows, piece * PATHS : (piece + 1) * PATHS],
+                    out[rows, first // STEPS : (first + entries) // STEPS],
                     path[:].rearrange("p t l -> p (t l)"),
                 )

@@ -5,7 +5,8 @@ NODES = 1024
 WORDS = 256
 ENTRIES = 1024
 STEPS = 4
-PIECE = (512, 256)
+PIECE = 256
+PATHS = PIECE // STEPS
 
 FLOPS = 2 * P * WORDS * ENTRIES
 
@@ -20,48 +21,43 @@ def tile_huffmantree_kernel(tc, table, words, sgn, offs, out):
     nc = tc.nc
     with (
         tc.tile_pool(name="held", bufs=1) as held,
-        tc.tile_pool(name="work", bufs=6) as work,
-        tc.psum_pool(name="psum", bufs=6) as psum,
+        tc.tile_pool(name="work", bufs=8) as work,
+        tc.psum_pool(name="psum", bufs=8) as psum,
     ):
+        offsets = held.tile([P, ENTRIES // 16], U16, name="offsets")
+        nc.sync.dma_start(offsets[:], offs)
         nodes = held.tile([P, NODES], BF16, name="nodes")
         nc.sync.dma_start(nodes[:], table)
         vectors = held.tile([P, WORDS], BF16, name="vectors")
         nc.sync.dma_start(vectors[:], words)
-        offsets = held.tile([P, ENTRIES // 16], U16, name="offsets")
-        nc.sync.dma_start(offsets[:], offs)
 
         for block in range(WORDS // P):
             rows = slice(block * P, (block + 1) * P)
-            entries = PIECE[block]
-            paths = entries // STEPS
-            for first in range(0, ENTRIES, entries):
-                sign = work.tile([P, entries], F32, name="sign")
-                nc.sync.dma_start(sign[:], sgn[rows, first : first + entries])
+            for piece in range(ENTRIES // PIECE):
+                sign = work.tile([P, PIECE], F32, name="sign")
+                nc.sync.dma_start(sign[:], sgn[rows, piece * PIECE : (piece + 1) * PIECE])
 
-                score = psum.tile([P, entries], F32, name="score")
+                score = psum.tile([P, PIECE], F32, name="score")
                 nc.tensor.matmul(
                     score[:],
                     vectors[:, rows],
-                    nodes[:].indirect(offsets[:, first // 16 : (first + entries) // 16]),
+                    nodes[:].indirect(offsets[:, piece * (PIECE // 16) : (piece + 1) * (PIECE // 16)]),
                     start=True,
                     stop=True,
                 )
 
-                signed = work.tile([P, entries], F32, name="signed")
+                signed = work.tile([P, PIECE], F32, name="signed")
                 nc.vector.tensor_tensor(signed[:], score[:], sign[:], MULT)
 
-                prob = work.tile([P, paths, STEPS], F32, name="prob")
+                prob = work.tile([P, PATHS, STEPS], F32, name="prob")
                 nc.scalar.activation(prob[:].rearrange("p t l -> p (t l)"), signed[:], SIGMOID)
 
-                path = work.tile([P, paths, 1], F32, name="path")
-                if block == 0:
-                    half = work.tile([P, paths, 2], F32, name="half")
-                    nc.gpsimd.tensor_tensor(half[:], prob[:, :, 0:2], prob[:, :, 2:4], MULT)
-                    nc.gpsimd.tensor_tensor(path[:], half[:, :, 0:1], half[:, :, 1:2], MULT)
-                else:
-                    nc.vector.tensor_reduce(path[:], prob[:], mybir.AxisListType.X, MULT)
+                half = work.tile([P, PATHS, 2], F32, name="half")
+                nc.vector.tensor_tensor(half[:], prob[:, :, 0:2], prob[:, :, 2:4], MULT)
+                path = work.tile([P, PATHS, 1], F32, name="path")
+                nc.vector.tensor_tensor(path[:], half[:, :, 0:1], half[:, :, 1:2], MULT)
 
                 nc.sync.dma_start(
-                    out[rows, first // STEPS : (first + entries) // STEPS],
+                    out[rows, piece * PATHS : (piece + 1) * PATHS],
                     path[:].rearrange("p t l -> p (t l)"),
                 )

@@ -5,8 +5,11 @@ NODES = 1024
 WORDS = 256
 ENTRIES = 1024
 STEPS = 4
-PIECE = 256
+PIECE = 512
 PATHS = PIECE // STEPS
+PIECES = ENTRIES // PIECE
+GPSIMD_UNITS = 1
+WARMUPS = 3
 
 FLOPS = 2 * P * WORDS * ENTRIES
 
@@ -21,8 +24,8 @@ def tile_huffmantree_kernel(tc, table, words, sgn, offs, out):
     nc = tc.nc
     with (
         tc.tile_pool(name="held", bufs=1) as held,
-        tc.tile_pool(name="work", bufs=8) as work,
-        tc.psum_pool(name="psum", bufs=8) as psum,
+        tc.tile_pool(name="work", bufs=4) as work,
+        tc.psum_pool(name="psum", bufs=4) as psum,
     ):
         offsets = held.tile([P, ENTRIES // 16], U16, name="offsets")
         nc.sync.dma_start(offsets[:], offs)
@@ -31,9 +34,16 @@ def tile_huffmantree_kernel(tc, table, words, sgn, offs, out):
         vectors = held.tile([P, WORDS], BF16, name="vectors")
         nc.sync.dma_start(vectors[:], words)
 
+        zeros = held.tile([P, 512], BF16, name="zeros")
+        nc.vector.memset(zeros[:], 0.0)
+        unused = psum.tile([P, 512], F32, name="unused")
+        for _ in range(WARMUPS):
+            nc.tensor.matmul(unused[:], zeros[:, 0:P], zeros[:], start=True, stop=True)
+
         for block in range(WORDS // P):
             rows = slice(block * P, (block + 1) * P)
-            for piece in range(ENTRIES // PIECE):
+            for piece in range(PIECES):
+                unit = block * PIECES + piece
                 sign = work.tile([P, PIECE], F32, name="sign")
                 nc.sync.dma_start(sign[:], sgn[rows, piece * PIECE : (piece + 1) * PIECE])
 
@@ -52,10 +62,13 @@ def tile_huffmantree_kernel(tc, table, words, sgn, offs, out):
                 prob = work.tile([P, PATHS, STEPS], F32, name="prob")
                 nc.scalar.activation(prob[:].rearrange("p t l -> p (t l)"), signed[:], SIGMOID)
 
-                half = work.tile([P, PATHS, 2], F32, name="half")
-                nc.vector.tensor_tensor(half[:], prob[:, :, 0:2], prob[:, :, 2:4], MULT)
                 path = work.tile([P, PATHS, 1], F32, name="path")
-                nc.vector.tensor_tensor(path[:], half[:, :, 0:1], half[:, :, 1:2], MULT)
+                if unit < GPSIMD_UNITS:
+                    half = work.tile([P, PATHS, 2], F32, name="half")
+                    nc.gpsimd.tensor_tensor(half[:], prob[:, :, 0:2], prob[:, :, 2:4], MULT)
+                    nc.gpsimd.tensor_tensor(path[:], half[:, :, 0:1], half[:, :, 1:2], MULT)
+                else:
+                    nc.vector.tensor_reduce(path[:], prob[:], mybir.AxisListType.X, MULT)
 
                 nc.sync.dma_start(
                     out[rows, piece * PATHS : (piece + 1) * PATHS],

@@ -6,10 +6,10 @@ WORDS = 256
 ENTRIES = 1024
 STEPS = 4
 PIECE = 512
-PATHS = PIECE // STEPS
-PIECES = ENTRIES // PIECE
-GPSIMD_UNITS = 1
 WARMUPS = 3
+
+UNITS = [(0, 0, PIECE // 2), (0, PIECE // 2, PIECE // 2), (0, PIECE, PIECE), (1, 0, PIECE), (1, PIECE, PIECE)]
+GPSIMD_UNITS = 2
 
 FLOPS = 2 * P * WORDS * ENTRIES
 
@@ -24,7 +24,7 @@ def tile_huffmantree_kernel(tc, table, words, sgn, offs, out):
     nc = tc.nc
     with (
         tc.tile_pool(name="held", bufs=1) as held,
-        tc.tile_pool(name="work", bufs=4) as work,
+        tc.tile_pool(name="work", bufs=len(UNITS)) as work,
         tc.psum_pool(name="psum", bufs=4) as psum,
     ):
         offsets = held.tile([P, ENTRIES // 16], U16, name="offsets")
@@ -40,37 +40,36 @@ def tile_huffmantree_kernel(tc, table, words, sgn, offs, out):
         for _ in range(WARMUPS):
             nc.tensor.matmul(unused[:], zeros[:, 0:P], zeros[:], start=True, stop=True)
 
-        for block in range(WORDS // P):
+        for unit, (block, first, entries) in enumerate(UNITS):
             rows = slice(block * P, (block + 1) * P)
-            for piece in range(PIECES):
-                unit = block * PIECES + piece
-                sign = work.tile([P, PIECE], F32, name="sign")
-                nc.sync.dma_start(sign[:], sgn[rows, piece * PIECE : (piece + 1) * PIECE])
+            paths = entries // STEPS
+            sign = work.tile([P, entries], F32, name="sign")
+            nc.sync.dma_start(sign[:], sgn[rows, first : first + entries])
 
-                score = psum.tile([P, PIECE], F32, name="score")
-                nc.tensor.matmul(
-                    score[:],
-                    vectors[:, rows],
-                    nodes[:].indirect(offsets[:, piece * (PIECE // 16) : (piece + 1) * (PIECE // 16)]),
-                    start=True,
-                    stop=True,
-                )
+            score = psum.tile([P, entries], F32, name="score")
+            nc.tensor.matmul(
+                score[:],
+                vectors[:, rows],
+                nodes[:].indirect(offsets[:, first // 16 : (first + entries) // 16]),
+                start=True,
+                stop=True,
+            )
 
-                signed = work.tile([P, PIECE], F32, name="signed")
-                nc.vector.tensor_tensor(signed[:], score[:], sign[:], MULT)
+            signed = work.tile([P, entries], F32, name="signed")
+            nc.vector.tensor_tensor(signed[:], score[:], sign[:], MULT)
 
-                prob = work.tile([P, PATHS, STEPS], F32, name="prob")
-                nc.scalar.activation(prob[:].rearrange("p t l -> p (t l)"), signed[:], SIGMOID)
+            prob = work.tile([P, paths, STEPS], F32, name="prob")
+            nc.scalar.activation(prob[:].rearrange("p t l -> p (t l)"), signed[:], SIGMOID)
 
-                path = work.tile([P, PATHS, 1], F32, name="path")
-                if unit < GPSIMD_UNITS:
-                    half = work.tile([P, PATHS, 2], F32, name="half")
-                    nc.gpsimd.tensor_tensor(half[:], prob[:, :, 0:2], prob[:, :, 2:4], MULT)
-                    nc.gpsimd.tensor_tensor(path[:], half[:, :, 0:1], half[:, :, 1:2], MULT)
-                else:
-                    nc.vector.tensor_reduce(path[:], prob[:], mybir.AxisListType.X, MULT)
+            path = work.tile([P, paths, 1], F32, name="path")
+            if unit < GPSIMD_UNITS:
+                half = work.tile([P, paths, 2], F32, name="half")
+                nc.gpsimd.tensor_tensor(half[:], prob[:, :, 0:2], prob[:, :, 2:4], MULT)
+                nc.gpsimd.tensor_tensor(path[:], half[:, :, 0:1], half[:, :, 1:2], MULT)
+            else:
+                nc.vector.tensor_reduce(path[:], prob[:], mybir.AxisListType.X, MULT)
 
-                nc.sync.dma_start(
-                    out[rows, piece * PATHS : (piece + 1) * PATHS],
-                    path[:].rearrange("p t l -> p (t l)"),
-                )
+            nc.sync.dma_start(
+                out[rows, first // STEPS : (first + entries) // STEPS],
+                path[:].rearrange("p t l -> p (t l)"),
+            )

@@ -8,8 +8,8 @@ STEPS = 4
 PIECE = 512
 WARMUPS = 3
 
-UNITS = [(0, 0, PIECE // 2), (0, PIECE // 2, PIECE // 2), (0, PIECE, PIECE), (1, 0, PIECE), (1, PIECE, PIECE)]
-GPSIMD_UNITS = 2
+UNITS = [(0, 0, PIECE // 2), (0, PIECE // 2, PIECE // 2), (0, PIECE, PIECE), (1, 0, PIECE), (1, PIECE, PIECE // 2), (1, PIECE + PIECE // 2, PIECE // 2)]
+GPSIMD_UNITS = (0, 1)
 
 FLOPS = 2 * P * WORDS * ENTRIES
 
@@ -62,7 +62,7 @@ def tile_huffmantree_kernel(tc, table, words, sgn, offs, out):
             nc.scalar.activation(prob[:].rearrange("p t l -> p (t l)"), signed[:], SIGMOID)
 
             path = work.tile([P, paths, 1], F32, name="path")
-            if unit < GPSIMD_UNITS:
+            if unit in GPSIMD_UNITS:
                 half = work.tile([P, paths, 2], F32, name="half")
                 nc.gpsimd.tensor_tensor(half[:], prob[:, :, 0:2], prob[:, :, 2:4], MULT)
                 nc.gpsimd.tensor_tensor(path[:], half[:, :, 0:1], half[:, :, 1:2], MULT)

@@ -6,7 +6,6 @@ WORDS = 256
 ENTRIES = 1024
 STEPS = 4
 PIECE = 512
-WARMUPS = 3
 
 UNITS = [(0, 0, PIECE // 2), (0, PIECE // 2, PIECE // 2), (0, PIECE, PIECE), (1, 0, PIECE), (1, PIECE, PIECE // 2), (1, PIECE + PIECE // 2, PIECE // 2)]
 GPSIMD_UNITS = (0, 1)
@@ -34,11 +33,6 @@ def tile_huffmantree_kernel(tc, table, words, sgn, offs, out):
         vectors = held.tile([P, WORDS], BF16, name="vectors")
         nc.sync.dma_start(vectors[:], words)
 
-        zeros = held.tile([P, 512], BF16, name="zeros")
-        nc.vector.memset(zeros[:], 0.0)
-        unused = psum.tile([P, 512], F32, name="unused")
-        for _ in range(WARMUPS):
-            nc.tensor.matmul(unused[:], zeros[:, 0:P], zeros[:], start=True, stop=True)
 
         for unit, (block, first, entries) in enumerate(UNITS):
             rows = slice(block * P, (block + 1) * P)

@@ -6,8 +6,10 @@ WORDS = 256
 ENTRIES = 1024
 STEPS = 4
 PIECE = 512
+HALF = PIECE // 2
 
-UNITS = [(0, 0, PIECE // 2), (0, PIECE // 2, PIECE // 2), (0, PIECE, PIECE), (1, 0, PIECE), (1, PIECE, PIECE // 2), (1, PIECE + PIECE // 2, PIECE // 2)]
+LOADS = [(0, 0, HALF, 1), (0, HALF, HALF, 1), (0, PIECE, PIECE, 1), (1, 0, PIECE, 1), (1, PIECE, PIECE, 2)]
+UNITS = sum(load[3] for load in LOADS)
 GPSIMD_UNITS = (0, 1)
 
 FLOPS = 2 * P * WORDS * ENTRIES
@@ -23,7 +25,7 @@ def tile_huffmantree_kernel(tc, table, words, sgn, offs, out):
     nc = tc.nc
     with (
         tc.tile_pool(name="held", bufs=1) as held,
-        tc.tile_pool(name="work", bufs=len(UNITS)) as work,
+        tc.tile_pool(name="work", bufs=UNITS) as work,
         tc.psum_pool(name="psum", bufs=4) as psum,
     ):
         offsets = held.tile([P, ENTRIES // 16], U16, name="offsets")
@@ -33,37 +35,44 @@ def tile_huffmantree_kernel(tc, table, words, sgn, offs, out):
         vectors = held.tile([P, WORDS], BF16, name="vectors")
         nc.sync.dma_start(vectors[:], words)
 
-
-        for unit, (block, first, entries) in enumerate(UNITS):
+        unit = 0
+        for block, loaded_from, loaded, units in LOADS:
             rows = slice(block * P, (block + 1) * P)
+            signs = work.tile([P, loaded], F32, name="signs")
+            nc.sync.dma_start(signs[:], sgn[rows, loaded_from : loaded_from + loaded])
+
+            entries = loaded // units
             paths = entries // STEPS
-            sign = work.tile([P, entries], F32, name="sign")
-            nc.sync.dma_start(sign[:], sgn[rows, first : first + entries])
+            for cut in range(units):
+                first = loaded_from + cut * entries
 
-            score = psum.tile([P, entries], F32, name="score")
-            nc.tensor.matmul(
-                score[:],
-                vectors[:, rows],
-                nodes[:].indirect(offsets[:, first // 16 : (first + entries) // 16]),
-                start=True,
-                stop=True,
-            )
+                score = psum.tile([P, entries], F32, name="score")
+                nc.tensor.matmul(
+                    score[:],
+                    vectors[:, rows],
+                    nodes[:].indirect(offsets[:, first // 16 : (first + entries) // 16]),
+                    start=True,
+                    stop=True,
+                )
 
-            signed = work.tile([P, entries], F32, name="signed")
-            nc.vector.tensor_tensor(signed[:], score[:], sign[:], MULT)
+                signed = work.tile([P, entries], F32, name="signed")
+                nc.vector.tensor_tensor(
+                    signed[:], score[:], signs[:, cut * entries : (cut + 1) * entries], MULT
+                )
 
-            prob = work.tile([P, paths, STEPS], F32, name="prob")
-            nc.scalar.activation(prob[:].rearrange("p t l -> p (t l)"), signed[:], SIGMOID)
+                prob = work.tile([P, paths, STEPS], F32, name="prob")
+                nc.scalar.activation(prob[:].rearrange("p t l -> p (t l)"), signed[:], SIGMOID)
 
-            path = work.tile([P, paths, 1], F32, name="path")
-            if unit in GPSIMD_UNITS:
-                half = work.tile([P, paths, 2], F32, name="half")
-                nc.gpsimd.tensor_tensor(half[:], prob[:, :, 0:2], prob[:, :, 2:4], MULT)
-                nc.gpsimd.tensor_tensor(path[:], half[:, :, 0:1], half[:, :, 1:2], MULT)
-            else:
-                nc.vector.tensor_reduce(path[:], prob[:], mybir.AxisListType.X, MULT)
+                path = work.tile([P, paths, 1], F32, name="path")
+                if unit in GPSIMD_UNITS:
+                    half = work.tile([P, paths, 2], F32, name="half")
+                    nc.gpsimd.tensor_tensor(half[:], prob[:, :, 0:2], prob[:, :, 2:4], MULT)
+                    nc.gpsimd.tensor_tensor(path[:], half[:, :, 0:1], half[:, :, 1:2], MULT)
+                else:
+                    nc.vector.tensor_reduce(path[:], prob[:], mybir.AxisListType.X, MULT)
 
-            nc.sync.dma_start(
-                out[rows, first // STEPS : (first + entries) // STEPS],
-                path[:].rearrange("p t l -> p (t l)"),
-            )
+                nc.sync.dma_start(
+                    out[rows, first // STEPS : (first + entries) // STEPS],
+                    path[:].rearrange("p t l -> p (t l)"),
+                )
+                unit += 1

@@ -8,7 +8,8 @@ STEPS = 4
 PIECE = 512
 HALF = PIECE // 2
 
-LOADS = [(0, 0, HALF, 1), (0, HALF, HALF, 1), (0, PIECE, PIECE, 1), (1, 0, PIECE, 1), (1, PIECE, PIECE, 2)]
+REST = (ENTRIES - HALF) // 2
+LOADS = [(0, 0, HALF, 1), (0, HALF, REST, 1), (0, HALF + REST, REST, 1), (1, 0, PIECE, 1), (1, PIECE, PIECE, 2)]
 UNITS = sum(load[3] for load in LOADS)
 GPSIMD_UNITS = (0, 1)
 
@@ -57,7 +58,7 @@ def tile_huffmantree_kernel(tc, table, words, sgn, offs, out):
 
                 signed = work.tile([P, entries], F32, name="signed")
                 nc.vector.tensor_tensor(
-                    signed[:], score[:], signs[:, cut * entries : (cut + 1) * entries], MULT
+                    signed[:], signs[:, cut * entries : (cut + 1) * entries], score[:], MULT
                 )
 
                 prob = work.tile([P, paths, STEPS], F32, name="prob")

@@ -58,7 +58,7 @@ def tile_huffmantree_kernel(tc, table, words, sgn, offs, out):
 
                 signed = work.tile([P, entries], F32, name="signed")
                 nc.vector.tensor_tensor(
-                    signed[:], signs[:, cut * entries : (cut + 1) * entries], score[:], MULT
+                    signed[:], score[:], signs[:, cut * entries : (cut + 1) * entries], MULT
                 )
 
                 prob = work.tile([P, paths, STEPS], F32, name="prob")

@@ -9,9 +9,10 @@ PIECE = 512
 HALF = PIECE // 2
 
 REST = (ENTRIES - HALF) // 2
-LOADS = [(0, 0, HALF, 1), (0, HALF, REST, 1), (0, HALF + REST, REST, 1), (1, 0, PIECE, 1), (1, PIECE, PIECE, 2)]
+LOADS = [(0, 0, HALF, 1), (0, HALF, REST, 1), (0, HALF + REST, REST, 1), (1, 0, PIECE, 2), (1, PIECE, PIECE, 2)]
 UNITS = sum(load[3] for load in LOADS)
-GPSIMD_UNITS = (0, 1)
+GPSIMD_LOADS = 2
+LAST_CUTS = 2
 
 FLOPS = 2 * P * WORDS * ENTRIES
 
@@ -24,9 +25,11 @@ SIGMOID = mybir.ActivationFunctionType.Sigmoid
 
 def tile_huffmantree_kernel(tc, table, words, sgn, offs, out):
     nc = tc.nc
+    vector_writes = UNITS + len(LOADS) - GPSIMD_LOADS + LAST_CUTS - 1
     with (
         tc.tile_pool(name="held", bufs=1) as held,
-        tc.tile_pool(name="work", bufs=UNITS) as work,
+        tc.tile_pool(name="work", bufs=len(LOADS)) as work,
+        tc.tile_pool(name="vector", bufs=vector_writes) as vector,
         tc.psum_pool(name="psum", bufs=4) as psum,
     ):
         offsets = held.tile([P, ENTRIES // 16], U16, name="offsets")
@@ -36,44 +39,53 @@ def tile_huffmantree_kernel(tc, table, words, sgn, offs, out):
         vectors = held.tile([P, WORDS], BF16, name="vectors")
         nc.sync.dma_start(vectors[:], words)
 
-        unit = 0
-        for block, loaded_from, loaded, units in LOADS:
+        def store(block, first, path):
+            paths = path.shape[1]
+            nc.sync.dma_start(
+                out[block * P : (block + 1) * P, first // STEPS : first // STEPS + paths],
+                path[:].rearrange("p t l -> p (t l)"),
+            )
+
+        probs = []
+        for block, first, loaded, units in LOADS:
             rows = slice(block * P, (block + 1) * P)
             signs = work.tile([P, loaded], F32, name="signs")
-            nc.sync.dma_start(signs[:], sgn[rows, loaded_from : loaded_from + loaded])
+            nc.sync.dma_start(signs[:], sgn[rows, first : first + loaded])
 
+            prob = work.tile([P, loaded // STEPS, STEPS], F32, name="prob")
             entries = loaded // units
-            paths = entries // STEPS
-            for cut in range(units):
-                first = loaded_from + cut * entries
-
+            for cut in range(0, loaded, entries):
                 score = psum.tile([P, entries], F32, name="score")
                 nc.tensor.matmul(
                     score[:],
                     vectors[:, rows],
-                    nodes[:].indirect(offsets[:, first // 16 : (first + entries) // 16]),
+                    nodes[:].indirect(offsets[:, (first + cut) // 16 : (first + cut + entries) // 16]),
                     start=True,
                     stop=True,
                 )
 
-                signed = work.tile([P, entries], F32, name="signed")
-                nc.vector.tensor_tensor(
-                    signed[:], score[:], signs[:, cut * entries : (cut + 1) * entries], MULT
+                signed = vector.tile([P, entries], F32, name="signed", tag="vector")
+                nc.vector.tensor_tensor(signed[:], score[:], signs[:, cut : cut + entries], MULT)
+
+                nc.scalar.activation(
+                    prob[:, cut // STEPS : (cut + entries) // STEPS, :].rearrange("p t l -> p (t l)"),
+                    signed[:],
+                    SIGMOID,
                 )
+            probs.append((block, first, prob))
 
-                prob = work.tile([P, paths, STEPS], F32, name="prob")
-                nc.scalar.activation(prob[:].rearrange("p t l -> p (t l)"), signed[:], SIGMOID)
+        for block, first, prob in probs[:GPSIMD_LOADS]:
+            paths = prob.shape[1]
+            half = work.tile([P, paths, 2], F32, name="half")
+            nc.gpsimd.tensor_tensor(half[:], prob[:, :, 0:2], prob[:, :, 2:4], MULT)
+            path = work.tile([P, paths, 1], F32, name="path_by_gpsimd")
+            nc.gpsimd.tensor_tensor(path[:], half[:, :, 0:1], half[:, :, 1:2], MULT)
+            store(block, first, path)
 
-                path = work.tile([P, paths, 1], F32, name="path")
-                if unit in GPSIMD_UNITS:
-                    half = work.tile([P, paths, 2], F32, name="half")
-                    nc.gpsimd.tensor_tensor(half[:], prob[:, :, 0:2], prob[:, :, 2:4], MULT)
-                    nc.gpsimd.tensor_tensor(path[:], half[:, :, 0:1], half[:, :, 1:2], MULT)
-                else:
-                    nc.vector.tensor_reduce(path[:], prob[:], mybir.AxisListType.X, MULT)
-
-                nc.sync.dma_start(
-                    out[rows, first // STEPS : (first + entries) // STEPS],
-                    path[:].rearrange("p t l -> p (t l)"),
-                )
-                unit += 1
+        for block, first, prob in probs[GPSIMD_LOADS:]:
+            cuts = LAST_CUTS if prob is probs[-1][2] else 1
+            paths = prob.shape[1] // cuts
+            for cut in range(0, prob.shape[1], paths):
+                path = vector.tile([P, paths, 1], F32, name="path", tag="vector")
+                nc.vector.tensor_reduce(path[:], prob[:, cut : cut + paths, :], mybir.AxisListType.X, MULT)
+                store(block, first + cut * STEPS, path)

@@ -7,12 +7,18 @@ ENTRIES = 1024
 STEPS = 4
 PIECE = 512
 HALF = PIECE // 2
+QUARTER = PIECE // 4
 
 REST = (ENTRIES - HALF) // 2
-LOADS = [(0, 0, HALF, 1), (0, HALF, REST, 1), (0, HALF + REST, REST, 1), (1, 0, PIECE, 2), (1, PIECE, PIECE, 2)]
-UNITS = sum(load[3] for load in LOADS)
+LOADS = [
+    (0, 0, (HALF,), (HALF,)),
+    (0, HALF, (REST,), (REST,)),
+    (0, HALF + REST, (REST,), (REST,)),
+    (1, 0, (HALF, HALF), (PIECE,)),
+    (1, PIECE, (HALF, QUARTER, QUARTER), (HALF + QUARTER, QUARTER)),
+]
 GPSIMD_LOADS = 2
-LAST_CUTS = 2
+VECTOR_TILES = sum(len(load[2]) for load in LOADS) + sum(len(load[3]) for load in LOADS[GPSIMD_LOADS:])
 
 FLOPS = 2 * P * WORDS * ENTRIES
 
@@ -25,17 +31,16 @@ SIGMOID = mybir.ActivationFunctionType.Sigmoid
 
 def tile_huffmantree_kernel(tc, table, words, sgn, offs, out):
     nc = tc.nc
-    vector_writes = UNITS + len(LOADS) - GPSIMD_LOADS + LAST_CUTS - 1
     with (
         tc.tile_pool(name="held", bufs=1) as held,
         tc.tile_pool(name="work", bufs=len(LOADS)) as work,
-        tc.tile_pool(name="vector", bufs=vector_writes) as vector,
+        tc.tile_pool(name="vector", bufs=VECTOR_TILES) as vector,
         tc.psum_pool(name="psum", bufs=4) as psum,
     ):
-        offsets = held.tile([P, ENTRIES // 16], U16, name="offsets")
-        nc.sync.dma_start(offsets[:], offs)
         nodes = held.tile([P, NODES], BF16, name="nodes")
         nc.sync.dma_start(nodes[:], table)
+        offsets = held.tile([P, ENTRIES // 16], U16, name="offsets")
+        nc.sync.dma_start(offsets[:], offs)
         vectors = held.tile([P, WORDS], BF16, name="vectors")
         nc.sync.dma_start(vectors[:], words)
 
@@ -47,45 +52,51 @@ def tile_huffmantree_kernel(tc, table, words, sgn, offs, out):
             )
 
         probs = []
-        for block, first, loaded, units in LOADS:
+        for block, first, units, products in LOADS:
             rows = slice(block * P, (block + 1) * P)
+            loaded = sum(units)
             signs = work.tile([P, loaded], F32, name="signs")
             nc.sync.dma_start(signs[:], sgn[rows, first : first + loaded])
 
             prob = work.tile([P, loaded // STEPS, STEPS], F32, name="prob")
-            entries = loaded // units
-            for cut in range(0, loaded, entries):
+            begin = 0
+            for entries in units:
+                end = begin + entries
                 score = psum.tile([P, entries], F32, name="score")
                 nc.tensor.matmul(
                     score[:],
                     vectors[:, rows],
-                    nodes[:].indirect(offsets[:, (first + cut) // 16 : (first + cut + entries) // 16]),
+                    nodes[:].indirect(offsets[:, (first + begin) // 16 : (first + end) // 16]),
                     start=True,
                     stop=True,
                 )
 
                 signed = vector.tile([P, entries], F32, name="signed", tag="vector")
-                nc.vector.tensor_tensor(signed[:], score[:], signs[:, cut : cut + entries], MULT)
+                nc.vector.tensor_tensor(signed[:], score[:], signs[:, begin:end], MULT)
 
                 nc.scalar.activation(
-                    prob[:, cut // STEPS : (cut + entries) // STEPS, :].rearrange("p t l -> p (t l)"),
+                    prob[:, begin // STEPS : end // STEPS, :].rearrange("p t l -> p (t l)"),
                     signed[:],
                     SIGMOID,
                 )
-            probs.append((block, first, prob))
+                begin = end
+            probs.append(prob)
 
-        for block, first, prob in probs[:GPSIMD_LOADS]:
+        for (block, first, units, products), prob in zip(LOADS[:GPSIMD_LOADS], probs[:GPSIMD_LOADS]):
             paths = prob.shape[1]
-            half = work.tile([P, paths, 2], F32, name="half")
+            half = work.tile([P, paths, 2], F32, name="half", tag="gpsimd")
             nc.gpsimd.tensor_tensor(half[:], prob[:, :, 0:2], prob[:, :, 2:4], MULT)
-            path = work.tile([P, paths, 1], F32, name="path_by_gpsimd")
+            path = work.tile([P, paths, 1], F32, name="path_by_gpsimd", tag="gpsimd")
             nc.gpsimd.tensor_tensor(path[:], half[:, :, 0:1], half[:, :, 1:2], MULT)
             store(block, first, path)
 
-        for block, first, prob in probs[GPSIMD_LOADS:]:
-            cuts = LAST_CUTS if prob is probs[-1][2] else 1
-            paths = prob.shape[1] // cuts
-            for cut in range(0, prob.shape[1], paths):
-                path = vector.tile([P, paths, 1], F32, name="path", tag="vector")
-                nc.vector.tensor_reduce(path[:], prob[:, cut : cut + paths, :], mybir.AxisListType.X, MULT)
-                store(block, first + cut * STEPS, path)
+        for (block, first, units, products), prob in zip(LOADS[GPSIMD_LOADS:], probs[GPSIMD_LOADS:]):
+            begin = 0
+            for entries in products:
+                end = begin + entries
+                path = vector.tile([P, entries // STEPS, 1], F32, name="path", tag="vector")
+                nc.vector.tensor_reduce(
+                    path[:], prob[:, begin // STEPS : end // STEPS, :], mybir.AxisListType.X, MULT
+                )
+                store(block, first + begin, path)
+                begin = end

import concourse.mybir as mybir

P = 128
NODES = 1024
WORDS = 256
ENTRIES = 1024
STEPS = 4
PIECE = 512
HALF = PIECE // 2
QUARTER = PIECE // 4

REST = (ENTRIES - HALF) // 2
LOADS = [
    (0, 0, (HALF,), (HALF,)),
    (0, HALF, (REST,), (REST,)),
    (0, HALF + REST, (REST,), (REST,)),
    (1, 0, (HALF, HALF), (PIECE,)),
    (1, PIECE, (HALF, QUARTER, QUARTER), (HALF + QUARTER, QUARTER)),
]
GPSIMD_LOADS = 2
VECTOR_TILES = sum(len(load[2]) for load in LOADS) + sum(len(load[3]) for load in LOADS[GPSIMD_LOADS:])

FLOPS = 2 * P * WORDS * ENTRIES

BF16 = mybir.dt.bfloat16
F32 = mybir.dt.float32
U16 = mybir.dt.uint16
MULT = mybir.AluOpType.mult
SIGMOID = mybir.ActivationFunctionType.Sigmoid


def tile_huffmantree_kernel(tc, table, words, sgn, offs, out):
    nc = tc.nc
    with (
        tc.tile_pool(name="held", bufs=1) as held,
        tc.tile_pool(name="work", bufs=len(LOADS)) as work,
        tc.tile_pool(name="vector", bufs=VECTOR_TILES) as vector,
        tc.psum_pool(name="psum", bufs=4) as psum,
    ):
        nodes = held.tile([P, NODES], BF16, name="nodes")
        nc.sync.dma_start(nodes[:], table)
        offsets = held.tile([P, ENTRIES // 16], U16, name="offsets")
        nc.sync.dma_start(offsets[:], offs)
        vectors = held.tile([P, WORDS], BF16, name="vectors")
        nc.sync.dma_start(vectors[:], words)

        def store(block, first, path):
            paths = path.shape[1]
            nc.sync.dma_start(
                out[block * P : (block + 1) * P, first // STEPS : first // STEPS + paths],
                path[:].rearrange("p t l -> p (t l)"),
            )

        probs = []
        for block, first, units, products in LOADS:
            rows = slice(block * P, (block + 1) * P)
            loaded = sum(units)
            signs = work.tile([P, loaded], F32, name="signs")
            nc.sync.dma_start(signs[:], sgn[rows, first : first + loaded])

            prob = work.tile([P, loaded // STEPS, STEPS], F32, name="prob")
            begin = 0
            for entries in units:
                end = begin + entries
                score = psum.tile([P, entries], F32, name="score")
                nc.tensor.matmul(
                    score[:],
                    vectors[:, rows],
                    nodes[:].indirect(offsets[:, (first + begin) // 16 : (first + end) // 16]),
                    start=True,
                    stop=True,
                )

                signed = vector.tile([P, entries], F32, name="signed", tag="vector")
                nc.vector.tensor_tensor(signed[:], score[:], signs[:, begin:end], MULT)

                nc.scalar.activation(
                    prob[:, begin // STEPS : end // STEPS, :].rearrange("p t l -> p (t l)"),
                    signed[:],
                    SIGMOID,
                )
                begin = end
            probs.append(prob)

        for (block, first, units, products), prob in zip(LOADS[:GPSIMD_LOADS], probs[:GPSIMD_LOADS]):
            paths = prob.shape[1]
            half = work.tile([P, paths, 2], F32, name="half", tag="gpsimd")
            nc.gpsimd.tensor_tensor(half[:], prob[:, :, 0:2], prob[:, :, 2:4], MULT)
            path = work.tile([P, paths, 1], F32, name="path_by_gpsimd", tag="gpsimd")
            nc.gpsimd.tensor_tensor(path[:], half[:, :, 0:1], half[:, :, 1:2], MULT)
            store(block, first, path)

        for (block, first, units, products), prob in zip(LOADS[GPSIMD_LOADS:], probs[GPSIMD_LOADS:]):
            begin = 0
            for entries in products:
                end = begin + entries
                path = vector.tile([P, entries // STEPS, 1], F32, name="path", tag="vector")
                nc.vector.tensor_reduce(
                    path[:], prob[:, begin // STEPS : end // STEPS, :], mybir.AxisListType.X, MULT
                )
                store(block, first + begin, path)
                begin = end
